import numpy as np
import ml_dtypes


def mxq(x, axis, fmt="e4m3"):
    dtype, down = {"e4m3": (ml_dtypes.float8_e4m3fn, 7), "e5m2": (ml_dtypes.float8_e5m2, 14)}[fmt]
    v = np.moveaxis(np.asarray(x, np.float32).astype(ml_dtypes.bfloat16).astype(np.float64), axis, -1)
    blocks = v.reshape(v.shape[:-1] + (-1, 32))
    amax = np.abs(blocks).max(-1, keepdims=True)
    byte = np.maximum(np.where(amax > 0, np.frexp(amax)[1] - 1 + 127, 0) - down, 1)
    scale = np.exp2(byte - 127.0)
    codes = (blocks / scale).astype(np.float32).astype(dtype).astype(np.float64)
    return np.moveaxis((codes * scale).reshape(v.shape), -1, axis)


WIDE = False


def mx_kscale(k):
    if not WIDE:
        return np.ones(k)
    levels = np.array([10, -10, 5, -5, 0])
    a = np.random.permutation(np.resize(levels, k // 512 * 4)).reshape(k // 512, 4)
    idx = np.arange(k)
    return np.exp2(a[idx // 512, idx % 128 // 32])


BF16 = ml_dtypes.bfloat16


def bf(x):
    return np.asarray(x, np.float32).astype(BF16)


def f64(x):
    return np.asarray(x).astype(np.float64)


B, N, D, H = 12, 512, 512, 2048


def setup_inputs():
    s = mx_kscale(D)
    return {"xwx": bf(np.abs(np.random.standard_normal((B, N, N))) * 2.0),
            "inp": bf(np.random.standard_normal((B, N, D)) / np.sqrt(N) * s),
            "V": bf(np.random.standard_normal((D, D)) * 1.5 * np.sqrt(N / D) / s[None, :]),
            "x": bf(np.random.standard_normal((B, N, D)))}


def reference(xwx, inp, V, x):
    u = mxq(f64(V), 1, "e4m3") @ mxq(f64(inp), 2, "e4m3").transpose(0, 2, 1)
    vx = np.sqrt(np.square(u) + 1e-8)
    sc = f64(xwx)
    e = np.exp(sc - sc.max(-1, keepdims=True))
    t = (mxq(e, 2, "e4m3") @ mxq(vx, 2, "e4m3").transpose(0, 2, 1)) / e.sum(-1, keepdims=True)
    return f64(x) + t

@@ -1,0 +1,296 @@
+from contextlib import ExitStack
+
+import concourse.mybir as mybir
+from concourse.masks import make_identity
+
+BF16 = mybir.dt.bfloat16
+F32 = mybir.dt.float32
+U32 = mybir.dt.uint32
+U8 = mybir.dt.uint8
+FP8X4 = mybir.dt.float8_e4m3fn_x4
+ACT = mybir.ActivationFunctionType
+ALU = mybir.AluOpType
+AXIS = mybir.AxisListType
+
+IMAGES = 12
+SIDE = 512
+P = 128
+PACK = 4
+TILES = SIDE // P
+HALVES = 2
+PER_HALF = TILES // HALVES
+IMAGE_COLS = TILES * SIDE
+EPS = 1e-8
+SCORE_BUFFERS = 4
+
+FLOPS = IMAGES * 2 * (2 * SIDE * SIDE * SIDE)
+
+
+def tile_quantumattentionblock_pb_t_kernel(tc, xwx, inp, V, x, out):
+    nc = tc.nc
+    with ExitStack() as ctx:
+        ctx.enter_context(tc.manual_schedule())
+        keep = ctx.enter_context(tc.tile_pool(name="keep", bufs=1))
+        resident = ctx.enter_context(tc.tile_pool(name="resident", bufs=IMAGES))
+        ring4 = ctx.enter_context(tc.tile_pool(name="ring4", bufs=SCORE_BUFFERS))
+        ring3 = ctx.enter_context(tc.tile_pool(name="ring3", bufs=3))
+        ring2 = ctx.enter_context(tc.tile_pool(name="ring2", bufs=2))
+        words_psum = ctx.enter_context(tc.psum_pool(name="words_psum", bufs=HALVES))
+        u_psum = ctx.enter_context(tc.psum_pool(name="u_psum", bufs=TILES))
+        turn_psum = ctx.enter_context(tc.psum_pool(name="turn_psum", bufs=2))
+
+        ident_bf16 = keep.tile([P, P], BF16)
+        make_identity(nc, ident_bf16[:])
+        ident_f32 = keep.tile([P, P], F32)
+        make_identity(nc, ident_f32[:])
+        eps = keep.tile([P, 1], F32)
+        nc.vector.memset(eps[:], EPS)
+
+        v_rows = keep.tile([P, IMAGE_COLS], BF16)
+        v_codes = keep.tile([P, SIDE], U32, align_bytes=64)
+        v_scales = keep.tile([P, SIDE], U8, align_bytes=64)
+        e_codes = keep.tile([P, IMAGES, SIDE], U32, align_bytes=64)
+        e_scales = keep.tile([P, IMAGES, SIDE], U8, align_bytes=64)
+
+        scores, folded, neg_max, probs, row_sum, inv_sum = {}, {}, {}, {}, {}, {}
+        probs_t, probs_grouped = {}, {}
+        inp_rows, x_rows, inp_words, inp_grouped, inp_mx = {}, {}, {}, {}, {}
+        u_banks, squares, vx_grouped, vx_mx = {}, {}, {}, {}
+
+        def live(b):
+            return 0 <= b < IMAGES
+
+        def load_scores(b):
+            rows = ring4.tile([P, TILES, SIDE], BF16, tag="scores")
+            nc.sync.dma_start(out=rows[:], in_=xwx[b].rearrange("(p a) n -> p a n", a=TILES))
+            scores[b] = rows
+
+        def load_residual(b):
+            rows = resident.tile([P, TILES, SIDE], BF16, tag="x_rows")
+            nc.sync.dma_start(out=rows[:], in_=x[b].rearrange("(p a) d -> p a d", a=TILES))
+            x_rows[b] = rows
+
+        def load_k_last(rows, matrix):
+            nc.sync.dma_start(
+                out=rows[:].rearrange("p (j f) -> p j f", j=TILES),
+                in_=matrix.rearrange("(j p) f -> p j f", p=P),
+            )
+
+        def load_embeddings(b):
+            rows = resident.tile([P, IMAGE_COLS], BF16, tag="inp_rows")
+            load_k_last(rows, inp[b])
+            inp_rows[b] = rows
+
+        def fold_first(b):
+            half = ring2.tile([P, TILES, SIDE // 2], BF16, tag="fold_half")
+            nc.vector.tensor_tensor(
+                out=half[:], in0=scores[b][:, :, : SIDE // 2], in1=scores[b][:, :, SIDE // 2 :], op=ALU.max
+            )
+            folded[b] = half
+
+        def fold_second(b):
+            quarter = ring2.tile([P, TILES, SIDE // 4], BF16, tag="fold_quarter")
+            nc.vector.tensor_tensor(
+                out=quarter[:], in0=folded[b][:, :, : SIDE // 4], in1=folded[b][:, :, SIDE // 4 :], op=ALU.max
+            )
+            folded[b] = quarter
+
+        def negated_row_max(b):
+            negated = ring3.tile([P, TILES], F32, tag="neg_max")
+            nc.vector.tensor_reduce(out=negated[:], in_=folded[b][:], axis=AXIS.X, op=ALU.max, negate=True)
+            neg_max[b] = negated
+
+        def exponentials(b, a):
+            if a == 0:
+                e_rows = ring2.tile([P, TILES, SIDE], BF16, tag="probs")
+                probs[b] = e_rows
+                sums = ring3.tile([P, TILES], F32, tag="row_sum")
+                row_sum[b] = sums
+            nc.scalar.activation(
+                out=probs[b][:, a, :],
+                in_=scores[b][:, a, :],
+                func=ACT.Exp,
+                bias=neg_max[b][:, a : a + 1],
+                accum_out=row_sum[b][:, a : a + 1],
+            )
+
+        def transpose_probs(b, a):
+            h = a // PER_HALF
+            if a % PER_HALF == 0:
+                bank = turn_psum.tile([P, PER_HALF, PACK, P], BF16, tag="turn")
+                probs_t[b, h] = bank
+            for j in range(PACK):
+                nc.tensor.transpose(
+                    probs_t[b, h][:, a % PER_HALF, j, :], probs[b][:, a, j * P : (j + 1) * P], ident_bf16[:]
+                )
+
+        def regroup_probs(b, h):
+            grouped = ring4.tile([P, PER_HALF, P, PACK], BF16, tag="probs_grouped", align_bytes=64)
+            hopping = probs_t[b, h][:].rearrange("p a j q -> p a q j")
+            if h == 0:
+                nc.vector.tensor_copy(out=grouped[:], in_=hopping)
+            else:
+                nc.scalar.copy(out=grouped[:], in_=hopping)
+            probs_grouped[b, h] = grouped
+
+        def quantise_probs(b, h):
+            cols = slice(h * PER_HALF * P, (h + 1) * PER_HALF * P)
+            nc.vector.quantize_mx(
+                out=e_codes[:, b, cols].bitcast(FP8X4),
+                scales=e_scales[:, b, cols],
+                in_=probs_grouped[b, h][:].rearrange("p a q j -> p (a q j)"),
+            )
+
+        def invert_row_sum(b):
+            inverse = resident.tile([P, TILES], F32, tag="inv_sum")
+            nc.vector.reciprocal(out=inverse[:], in_=row_sum[b][:])
+            inv_sum[b] = inverse
+
+        def softmax_step(s):
+            if live(s + 1):
+                fold_first(s + 1)
+            if live(s - 1):
+                invert_row_sum(s - 1)
+                quantise_probs(s - 1, 0)
+            if live(s + 1):
+                fold_second(s + 1)
+            if live(s):
+                exponentials(s, 0)
+                transpose_probs(s, 0)
+            if live(s - 1):
+                regroup_probs(s - 1, 1)
+                quantise_probs(s - 1, 1)
+            if live(s + 1):
+                negated_row_max(s + 1)
+            if live(s):
+                for a in range(1, TILES):
+                    exponentials(s, a)
+                    transpose_probs(s, a)
+                regroup_probs(s, 0)
+                load_embeddings(s)
+                load_residual(s)
+            if live(s) and live(s + SCORE_BUFFERS):
+                load_scores(s + SCORE_BUFFERS)
+
+        def transpose_words(rows):
+            words = rows[:].bitcast(F32)
+            banks = []
+            for h in range(HALVES):
+                bank = words_psum.tile([P, PER_HALF, 2, P], F32, tag="words")
+                for i in range(PER_HALF):
+                    for u in range(2):
+                        first = ((h * PER_HALF + i) * 2 + u) * P
+                        nc.tensor.transpose(bank[:, i, u, :], words[:, first : first + P], ident_f32[:])
+                banks.append(bank)
+            return banks
+
+        def regroup_words(banks):
+            grouped = ring2.tile([P, IMAGE_COLS], BF16, tag="words_grouped", align_bytes=64)
+            as_words = grouped[:].bitcast(F32).rearrange("p (h i r u) -> p h i r u", h=HALVES, i=PER_HALF, u=2)
+            for h in range(HALVES):
+                nc.vector.tensor_copy(out=as_words[:, h], in_=banks[h][:].rearrange("p i u r -> p i r u"))
+            return grouped
+
+        def prepare_v():
+            grouped = regroup_words(transpose_words(v_rows))
+            nc.vector.quantize_mx(out=v_codes[:].bitcast(FP8X4), scales=v_scales[:], in_=grouped[:])
+
+        def quantise_embeddings(b):
+            codes = ring2.tile([P, SIDE], U32, tag="inp_codes", align_bytes=64)
+            scales = ring2.tile([P, SIDE], U8, tag="inp_scales", align_bytes=64)
+            nc.vector.quantize_mx(out=codes[:].bitcast(FP8X4), scales=scales[:], in_=inp_grouped[b][:])
+            inp_mx[b] = (codes, scales)
+
+        def project(b):
+            codes, scales = inp_mx[b]
+            banks = []
+            for c in range(TILES):
+                bank = u_psum.tile([P, PACK, P], F32, tag="u")
+                for j in range(PACK):
+                    nc.tensor.matmul_mx(
+                        out=bank[:, j, :],
+                        lhsT=codes[:, j * P : (j + 1) * P].bitcast(FP8X4),
+                        lhsT_scale=scales[:, j * P : (j + 1) * P],
+                        rhs=v_codes[:, c * P : (c + 1) * P].bitcast(FP8X4),
+                        rhs_scale=v_scales[:, c * P : (c + 1) * P],
+                        start=True,
+                        stop=True,
+                    )
+                banks.append(bank)
+            u_banks[b] = banks
+
+        def square(b):
+            squared = ring2.tile([P, TILES, P, PACK], F32, tag="squares")
+            for c in range(TILES):
+                nc.scalar.activation(
+                    out=squared[:, c], in_=u_banks[b][c][:].rearrange("p j d -> p d j"), func=ACT.Square
+                )
+            squares[b] = squared
+
+        def root(b):
+            grouped = ring2.tile([P, HALVES, IMAGE_COLS // HALVES], BF16, tag="vx_grouped", align_bytes=64)
+            flat = squares[b][:].rearrange("p (h c) d j -> p h (c d j)", h=HALVES)
+            for h in range(HALVES):
+                nc.scalar.activation(out=grouped[:, h, :], in_=flat[:, h, :], func=ACT.Sqrt, bias=eps[:, 0:1])
+            vx_grouped[b] = grouped
+
+        def quantise_values(b):
+            codes = ring2.tile([P, SIDE], U32, tag="vx_codes", align_bytes=64)
+            scales = ring2.tile([P, SIDE], U8, tag="vx_scales", align_bytes=64)
+            nc.vector.quantize_mx(
+                out=codes[:].bitcast(FP8X4), scales=scales[:], in_=vx_grouped[b][:].rearrange("p h c -> p (h c)")
+            )
+            vx_mx[b] = (codes, scales)
+
+        def attend(b):
+            codes, scales = vx_mx[b]
+            out_rows = out[b].rearrange("(p a) d -> p a d", a=TILES)
+            for h in range(HALVES):
+                result = ring4.tile([P, PER_HALF, SIDE], F32, tag="result")
+                for i in range(PER_HALF):
+                    a = h * PER_HALF + i
+                    bank = turn_psum.tile([P, SIDE], F32, tag="turn")
+                    nc.tensor.matmul_mx(
+                        out=bank[:],
+                        lhsT=e_codes[:, b, a * P : (a + 1) * P].bitcast(FP8X4),
+                        lhsT_scale=e_scales[:, b, a * P : (a + 1) * P],
+                        rhs=codes[:].bitcast(FP8X4),
+                        rhs_scale=scales[:],
+                        start=True,
+                        stop=True,
+                    )
+                    nc.vector.scalar_tensor_tensor(
+                        out=result[:, i, :],
+                        in0=bank[:],
+                        scalar=inv_sum[b][:, a : a + 1],
+                        in1=x_rows[b][:, a, :],
+                        op0=ALU.mult,
+                        op1=ALU.add,
+                    )
+                nc.sync.dma_start(out=out_rows[:, h * PER_HALF : (h + 1) * PER_HALF, :], in_=result[:])
+
+        def value_step(t):
+            if live(t):
+                square(t)
+                root(t)
+            if live(t - 1):
+                quantise_values(t - 1)
+            if live(t + 1):
+                quantise_embeddings(t + 1)
+            if live(t - 1):
+                attend(t - 1)
+            if live(t + 1):
+                project(t + 1)
+            if live(t + 2):
+                inp_grouped[t + 2] = regroup_words(inp_words[t + 2])
+            if live(t + 3):
+                inp_words[t + 3] = transpose_words(inp_rows[t + 3])
+
+        for b in range(SCORE_BUFFERS):
+            load_scores(b)
+        load_k_last(v_rows, V)
+        for s in range(-1, 2 * IMAGES + 1):
+            softmax_step(s)
+            if s == 0:
+                prepare_v()
+            value_step(s - IMAGES)

@@ -39,8 +39,6 @@ def tile_quantumattentionblock_pb_t_kernel(tc, xwx, inp, V, x, out):
         u_psum = ctx.enter_context(tc.psum_pool(name="u_psum", bufs=TILES))
         turn_psum = ctx.enter_context(tc.psum_pool(name="turn_psum", bufs=2))
 
-        ident_bf16 = keep.tile([P, P], BF16)
-        make_identity(nc, ident_bf16[:])
         ident_f32 = keep.tile([P, P], F32)
         make_identity(nc, ident_f32[:])
         eps = keep.tile([P, 1], F32)
@@ -53,7 +51,7 @@ def tile_quantumattentionblock_pb_t_kernel(tc, xwx, inp, V, x, out):
         e_scales = keep.tile([P, IMAGES, SIDE], U8, align_bytes=64)
 
         scores, folded, neg_max, probs, row_sum, inv_sum = {}, {}, {}, {}, {}, {}
-        probs_t, probs_grouped = {}, {}
+        probs_words, probs_grouped = {}, {}
         inp_rows, x_rows, inp_words, inp_grouped, inp_mx = {}, {}, {}, {}, {}
         u_banks, squares, vx_grouped, vx_mx = {}, {}, {}, {}
 
@@ -70,16 +68,32 @@ def tile_quantumattentionblock_pb_t_kernel(tc, xwx, inp, V, x, out):
             nc.sync.dma_start(out=rows[:], in_=x[b].rearrange("(p a) d -> p a d", a=TILES))
             x_rows[b] = rows
 
-        def load_k_last(rows, matrix):
-            nc.sync.dma_start(
-                out=rows[:].rearrange("p (j f) -> p j f", j=TILES),
-                in_=matrix.rearrange("(j p) f -> p j f", p=P),
-            )
-
         def load_embeddings(b):
             rows = resident.tile([P, IMAGE_COLS], BF16, tag="inp_rows")
-            load_k_last(rows, inp[b])
+            nc.sync.dma_start(
+                out=rows[:].rearrange("p (u c) -> p u c", u=2),
+                in_=inp[b].rearrange("(u p e) f -> p u (e f)", u=2, e=2),
+            )
             inp_rows[b] = rows
+
+        def load_v():
+            nc.sync.dma_start(
+                out=v_rows[:].rearrange("p (c f) -> p c f", c=TILES),
+                in_=V.rearrange("(c p) f -> p c f", p=P),
+            )
+
+        def transpose_words(rows, h, pool, tag):
+            words = rows[:].bitcast(F32)
+            bank = pool.tile([P, PER_HALF, 2, P], F32, tag=tag)
+            for i in range(PER_HALF):
+                for u in range(2):
+                    first = ((h * PER_HALF + i) * 2 + u) * P
+                    nc.tensor.transpose(bank[:, i, u, :], words[:, first : first + P], ident_f32[:])
+            return bank
+
+        def word_views(grouped, h, bank):
+            as_words = grouped[:].bitcast(F32).rearrange("p (h i r u) -> p h i r u", h=HALVES, i=PER_HALF, u=2)
+            return as_words[:, h], bank[:].rearrange("p i u r -> p i r u")
 
         def fold_first(b):
             half = ring2.tile([P, TILES, SIDE // 2], BF16, tag="fold_half")
@@ -102,43 +116,38 @@ def tile_quantumattentionblock_pb_t_kernel(tc, xwx, inp, V, x, out):
 
         def exponentials(b, a):
             if a == 0:
-                e_rows = ring2.tile([P, TILES, SIDE], BF16, tag="probs")
+                e_rows = ring2.tile([P, IMAGE_COLS], BF16, tag="probs")
                 probs[b] = e_rows
                 sums = ring3.tile([P, TILES], F32, tag="row_sum")
                 row_sum[b] = sums
             nc.scalar.activation(
-                out=probs[b][:, a, :],
+                out=probs[b][:, a * SIDE : (a + 1) * SIDE],
                 in_=scores[b][:, a, :],
                 func=ACT.Exp,
                 bias=neg_max[b][:, a : a + 1],
                 accum_out=row_sum[b][:, a : a + 1],
             )
 
-        def transpose_probs(b, a):
-            h = a // PER_HALF
-            if a % PER_HALF == 0:
-                bank = turn_psum.tile([P, PER_HALF, PACK, P], BF16, tag="turn")
-                probs_t[b, h] = bank
-            for j in range(PACK):
-                nc.tensor.transpose(
-                    probs_t[b, h][:, a % PER_HALF, j, :], probs[b][:, a, j * P : (j + 1) * P], ident_bf16[:]
-                )
+        def transpose_probs(b, h):
+            probs_words[b, h] = transpose_words(probs[b], h, turn_psum, "turn")
 
         def regroup_probs(b, h):
-            grouped = ring4.tile([P, PER_HALF, P, PACK], BF16, tag="probs_grouped", align_bytes=64)
-            hopping = probs_t[b, h][:].rearrange("p a j q -> p a q j")
             if h == 0:
-                nc.vector.tensor_copy(out=grouped[:], in_=hopping)
+                grouped = ring2.tile([P, IMAGE_COLS], BF16, tag="probs_grouped", align_bytes=64)
+                probs_grouped[b] = grouped
+            to_sbuf, from_psum = word_views(probs_grouped[b], h, probs_words[b, h])
+            if h == 0:
+                nc.vector.tensor_copy(out=to_sbuf, in_=from_psum)
             else:
-                nc.scalar.copy(out=grouped[:], in_=hopping)
-            probs_grouped[b, h] = grouped
+                nc.scalar.copy(out=to_sbuf, in_=from_psum)
 
         def quantise_probs(b, h):
-            cols = slice(h * PER_HALF * P, (h + 1) * PER_HALF * P)
+            words = slice(h * PER_HALF * P, (h + 1) * PER_HALF * P)
+            values = slice(h * PER_HALF * P * PACK, (h + 1) * PER_HALF * P * PACK)
             nc.vector.quantize_mx(
-                out=e_codes[:, b, cols].bitcast(FP8X4),
-                scales=e_scales[:, b, cols],
-                in_=probs_grouped[b, h][:].rearrange("p a q j -> p (a q j)"),
+                out=e_codes[:, b, words].bitcast(FP8X4),
+                scales=e_scales[:, b, words],
+                in_=probs_grouped[b][:, values],
             )
 
         def invert_row_sum(b):
@@ -156,43 +165,35 @@ def tile_quantumattentionblock_pb_t_kernel(tc, xwx, inp, V, x, out):
                 fold_second(s + 1)
             if live(s):
                 exponentials(s, 0)
-                transpose_probs(s, 0)
             if live(s - 1):
                 regroup_probs(s - 1, 1)
                 quantise_probs(s - 1, 1)
             if live(s + 1):
                 negated_row_max(s + 1)
             if live(s):
-                for a in range(1, TILES):
-                    exponentials(s, a)
-                    transpose_probs(s, a)
+                exponentials(s, 1)
+                transpose_probs(s, 0)
+                exponentials(s, 2)
+                exponentials(s, 3)
+                transpose_probs(s, 1)
                 regroup_probs(s, 0)
                 load_embeddings(s)
                 load_residual(s)
             if live(s) and live(s + SCORE_BUFFERS):
                 load_scores(s + SCORE_BUFFERS)
 
-        def transpose_words(rows):
-            words = rows[:].bitcast(F32)
-            banks = []
-            for h in range(HALVES):
-                bank = words_psum.tile([P, PER_HALF, 2, P], F32, tag="words")
-                for i in range(PER_HALF):
-                    for u in range(2):
-                        first = ((h * PER_HALF + i) * 2 + u) * P
-                        nc.tensor.transpose(bank[:, i, u, :], words[:, first : first + P], ident_f32[:])
-                banks.append(bank)
-            return banks
+        def transpose_rows(rows):
+            return [transpose_words(rows, h, words_psum, "words") for h in range(HALVES)]
 
-        def regroup_words(banks):
-            grouped = ring2.tile([P, IMAGE_COLS], BF16, tag="words_grouped", align_bytes=64)
-            as_words = grouped[:].bitcast(F32).rearrange("p (h i r u) -> p h i r u", h=HALVES, i=PER_HALF, u=2)
+        def regroup_rows(banks):
+            grouped = ring2.tile([P, IMAGE_COLS], BF16, tag="rows_grouped", align_bytes=64)
             for h in range(HALVES):
-                nc.vector.tensor_copy(out=as_words[:, h], in_=banks[h][:].rearrange("p i u r -> p i r u"))
+                to_sbuf, from_psum = word_views(grouped, h, banks[h])
+                nc.vector.tensor_copy(out=to_sbuf, in_=from_psum)
             return grouped
 
         def prepare_v():
-            grouped = regroup_words(transpose_words(v_rows))
+            grouped = regroup_rows(transpose_rows(v_rows))
             nc.vector.quantize_mx(out=v_codes[:].bitcast(FP8X4), scales=v_scales[:], in_=grouped[:])
 
         def quantise_embeddings(b):
@@ -282,13 +283,13 @@ def tile_quantumattentionblock_pb_t_kernel(tc, xwx, inp, V, x, out):
             if live(t + 1):
                 project(t + 1)
             if live(t + 2):
-                inp_grouped[t + 2] = regroup_words(inp_words[t + 2])
+                inp_grouped[t + 2] = regroup_rows(inp_words[t + 2])
             if live(t + 3):
-                inp_words[t + 3] = transpose_words(inp_rows[t + 3])
+                inp_words[t + 3] = transpose_rows(inp_rows[t + 3])
 
         for b in range(SCORE_BUFFERS):
             load_scores(b)
-        load_k_last(v_rows, V)
+        load_v()
         for s in range(-1, 2 * IMAGES + 1):
             softmax_step(s)
             if s == 0:

@@ -49,8 +49,10 @@ def tile_quantumattentionblock_pb_t_kernel(tc, xwx, inp, V, x, out):
         v_scales = keep.tile([P, SIDE], U8, align_bytes=64)
         e_codes = keep.tile([P, IMAGES, SIDE], U32, align_bytes=64)
         e_scales = keep.tile([P, IMAGES, SIDE], U8, align_bytes=64)
+        row_sum = keep.tile([P, IMAGES * TILES], F32)
+        inv_sum = keep.tile([P, IMAGES * TILES], F32)
 
-        scores, folded, neg_max, probs, row_sum, inv_sum = {}, {}, {}, {}, {}, {}
+        scores, folded, neg_max, probs = {}, {}, {}, {}
         probs_words, probs_grouped = {}, {}
         inp_rows, x_rows, inp_words, inp_grouped, inp_mx = {}, {}, {}, {}, {}
         u_banks, squares, vx_grouped, vx_mx = {}, {}, {}, {}
@@ -118,14 +120,12 @@ def tile_quantumattentionblock_pb_t_kernel(tc, xwx, inp, V, x, out):
             if a == 0:
                 e_rows = ring2.tile([P, IMAGE_COLS], BF16, tag="probs")
                 probs[b] = e_rows
-                sums = ring3.tile([P, TILES], F32, tag="row_sum")
-                row_sum[b] = sums
             nc.scalar.activation(
                 out=probs[b][:, a * SIDE : (a + 1) * SIDE],
                 in_=scores[b][:, a, :],
                 func=ACT.Exp,
                 bias=neg_max[b][:, a : a + 1],
-                accum_out=row_sum[b][:, a : a + 1],
+                accum_out=row_sum[:, TILES * b + a : TILES * b + a + 1],
             )
 
         def transpose_probs(b, h):
@@ -141,42 +141,32 @@ def tile_quantumattentionblock_pb_t_kernel(tc, xwx, inp, V, x, out):
             else:
                 nc.scalar.copy(out=to_sbuf, in_=from_psum)
 
-        def quantise_probs(b, h):
-            words = slice(h * PER_HALF * P, (h + 1) * PER_HALF * P)
-            values = slice(h * PER_HALF * P * PACK, (h + 1) * PER_HALF * P * PACK)
+        def quantise_probs(b):
             nc.vector.quantize_mx(
-                out=e_codes[:, b, words].bitcast(FP8X4),
-                scales=e_scales[:, b, words],
-                in_=probs_grouped[b][:, values],
+                out=e_codes[:, b, :].bitcast(FP8X4), scales=e_scales[:, b, :], in_=probs_grouped[b][:]
             )
-
-        def invert_row_sum(b):
-            inverse = resident.tile([P, TILES], F32, tag="inv_sum")
-            nc.vector.reciprocal(out=inverse[:], in_=row_sum[b][:])
-            inv_sum[b] = inverse
 
         def softmax_step(s):
             if live(s + 1):
                 fold_first(s + 1)
-            if live(s - 1):
-                invert_row_sum(s - 1)
-                quantise_probs(s - 1, 0)
+            if live(s - 2):
+                quantise_probs(s - 2)
             if live(s + 1):
                 fold_second(s + 1)
-            if live(s):
-                exponentials(s, 0)
             if live(s - 1):
-                regroup_probs(s - 1, 1)
-                quantise_probs(s - 1, 1)
+                regroup_probs(s - 1, 0)
             if live(s + 1):
                 negated_row_max(s + 1)
             if live(s):
+                exponentials(s, 0)
                 exponentials(s, 1)
                 transpose_probs(s, 0)
+            if live(s - 1):
+                regroup_probs(s - 1, 1)
+            if live(s):
                 exponentials(s, 2)
                 exponentials(s, 3)
                 transpose_probs(s, 1)
-                regroup_probs(s, 0)
                 load_embeddings(s)
                 load_residual(s)
             if live(s) and live(s + SCORE_BUFFERS):
@@ -202,10 +192,9 @@ def tile_quantumattentionblock_pb_t_kernel(tc, xwx, inp, V, x, out):
             nc.vector.quantize_mx(out=codes[:].bitcast(FP8X4), scales=scales[:], in_=inp_grouped[b][:])
             inp_mx[b] = (codes, scales)
 
-        def project(b):
+        def project(b, h):
             codes, scales = inp_mx[b]
-            banks = []
-            for c in range(TILES):
+            for c in range(h * PER_HALF, (h + 1) * PER_HALF):
                 bank = u_psum.tile([P, PACK, P], F32, tag="u")
                 for j in range(PACK):
                     nc.tensor.matmul_mx(
@@ -217,14 +206,13 @@ def tile_quantumattentionblock_pb_t_kernel(tc, xwx, inp, V, x, out):
                         start=True,
                         stop=True,
                     )
-                banks.append(bank)
-            u_banks[b] = banks
+                u_banks[b, c] = bank
 
         def square(b):
             squared = ring2.tile([P, TILES, P, PACK], F32, tag="squares")
             for c in range(TILES):
                 nc.scalar.activation(
-                    out=squared[:, c], in_=u_banks[b][c][:].rearrange("p j d -> p d j"), func=ACT.Square
+                    out=squared[:, c], in_=u_banks[b, c][:].rearrange("p j d -> p d j"), func=ACT.Square
                 )
             squares[b] = squared
 
@@ -243,32 +231,30 @@ def tile_quantumattentionblock_pb_t_kernel(tc, xwx, inp, V, x, out):
             )
             vx_mx[b] = (codes, scales)
 
-        def attend(b):
+        def attend(b, h):
             codes, scales = vx_mx[b]
             out_rows = out[b].rearrange("(p a) d -> p a d", a=TILES)
-            for h in range(HALVES):
-                result = ring4.tile([P, PER_HALF, SIDE], F32, tag="result")
-                for i in range(PER_HALF):
-                    a = h * PER_HALF + i
-                    bank = turn_psum.tile([P, SIDE], F32, tag="turn")
-                    nc.tensor.matmul_mx(
-                        out=bank[:],
-                        lhsT=e_codes[:, b, a * P : (a + 1) * P].bitcast(FP8X4),
-                        lhsT_scale=e_scales[:, b, a * P : (a + 1) * P],
-                        rhs=codes[:].bitcast(FP8X4),
-                        rhs_scale=scales[:],
-                        start=True,
-                        stop=True,
-                    )
-                    nc.vector.scalar_tensor_tensor(
-                        out=result[:, i, :],
-                        in0=bank[:],
-                        scalar=inv_sum[b][:, a : a + 1],
-                        in1=x_rows[b][:, a, :],
-                        op0=ALU.mult,
-                        op1=ALU.add,
-                    )
-                nc.sync.dma_start(out=out_rows[:, h * PER_HALF : (h + 1) * PER_HALF, :], in_=result[:])
+            for a in range(h * PER_HALF, (h + 1) * PER_HALF):
+                bank = turn_psum.tile([P, SIDE], F32, tag="turn")
+                nc.tensor.matmul_mx(
+                    out=bank[:],
+                    lhsT=e_codes[:, b, a * P : (a + 1) * P].bitcast(FP8X4),
+                    lhsT_scale=e_scales[:, b, a * P : (a + 1) * P],
+                    rhs=codes[:].bitcast(FP8X4),
+                    rhs_scale=scales[:],
+                    start=True,
+                    stop=True,
+                )
+                result = ring4.tile([P, SIDE], F32, tag="result")
+                nc.vector.scalar_tensor_tensor(
+                    out=result[:],
+                    in0=bank[:],
+                    scalar=inv_sum[:, TILES * b + a : TILES * b + a + 1],
+                    in1=x_rows[b][:, a, :],
+                    op0=ALU.mult,
+                    op1=ALU.add,
+                )
+                nc.sync.dma_start(out=out_rows[:, a, :], in_=result[:])
 
         def value_step(t):
             if live(t):
@@ -278,10 +264,11 @@ def tile_quantumattentionblock_pb_t_kernel(tc, xwx, inp, V, x, out):
                 quantise_values(t - 1)
             if live(t + 1):
                 quantise_embeddings(t + 1)
-            if live(t - 1):
-                attend(t - 1)
-            if live(t + 1):
-                project(t + 1)
+            for h in range(HALVES):
+                if live(t - 1):
+                    attend(t - 1, h)
+                if live(t + 1):
+                    project(t + 1, h)
             if live(t + 2):
                 inp_grouped[t + 2] = regroup_rows(inp_words[t + 2])
             if live(t + 3):
@@ -289,9 +276,12 @@ def tile_quantumattentionblock_pb_t_kernel(tc, xwx, inp, V, x, out):
 
         for b in range(SCORE_BUFFERS):
             load_scores(b)
-        load_v()
+            if b == 1:
+                load_v()
         for s in range(-1, 2 * IMAGES + 1):
             softmax_step(s)
             if s == 0:
                 prepare_v()
+            if s == IMAGES:
+                nc.vector.reciprocal(out=inv_sum[:], in_=row_sum[:])
             value_step(s - IMAGES)

@@ -21,7 +21,11 @@ HALVES = 2
 PER_HALF = TILES // HALVES
 IMAGE_COLS = TILES * SIDE
 EPS = 1e-8
-SCORE_BUFFERS = 4
+SCORE_BUFFERS = 6
+RESIDUAL_BUFFERS = 6
+RESIDUAL_STEP = 8
+VALUE_START = IMAGES - 1
+RESULT_BUFFERS = 8
 
 FLOPS = IMAGES * 2 * (2 * SIDE * SIDE * SIDE)
 
@@ -32,7 +36,9 @@ def tile_quantumattentionblock_pb_t_kernel(tc, xwx, inp, V, x, out):
         ctx.enter_context(tc.manual_schedule())
         keep = ctx.enter_context(tc.tile_pool(name="keep", bufs=1))
         resident = ctx.enter_context(tc.tile_pool(name="resident", bufs=IMAGES))
-        ring4 = ctx.enter_context(tc.tile_pool(name="ring4", bufs=SCORE_BUFFERS))
+        score_ring = ctx.enter_context(tc.tile_pool(name="score_ring", bufs=SCORE_BUFFERS))
+        residual_ring = ctx.enter_context(tc.tile_pool(name="residual_ring", bufs=RESIDUAL_BUFFERS))
+        result_ring = ctx.enter_context(tc.tile_pool(name="result_ring", bufs=RESULT_BUFFERS))
         ring3 = ctx.enter_context(tc.tile_pool(name="ring3", bufs=3))
         ring2 = ctx.enter_context(tc.tile_pool(name="ring2", bufs=2))
         words_psum = ctx.enter_context(tc.psum_pool(name="words_psum", bufs=HALVES))
@@ -61,12 +67,12 @@ def tile_quantumattentionblock_pb_t_kernel(tc, xwx, inp, V, x, out):
             return 0 <= b < IMAGES
 
         def load_scores(b):
-            rows = ring4.tile([P, TILES, SIDE], BF16, tag="scores")
+            rows = score_ring.tile([P, TILES, SIDE], BF16, tag="scores")
             nc.sync.dma_start(out=rows[:], in_=xwx[b].rearrange("(p a) n -> p a n", a=TILES))
             scores[b] = rows
 
         def load_residual(b):
-            rows = resident.tile([P, TILES, SIDE], BF16, tag="x_rows")
+            rows = residual_ring.tile([P, TILES, SIDE], BF16, tag="x_rows")
             nc.sync.dma_start(out=rows[:], in_=x[b].rearrange("(p a) d -> p a d", a=TILES))
             x_rows[b] = rows
 
@@ -131,12 +137,15 @@ def tile_quantumattentionblock_pb_t_kernel(tc, xwx, inp, V, x, out):
         def transpose_probs(b, h):
             probs_words[b, h] = transpose_words(probs[b], h, turn_psum, "turn")
 
+        def vector_regroups(b, h):
+            return h == 0 or b % 3 == 2
+
         def regroup_probs(b, h):
             if h == 0:
                 grouped = ring2.tile([P, IMAGE_COLS], BF16, tag="probs_grouped", align_bytes=64)
                 probs_grouped[b] = grouped
             to_sbuf, from_psum = word_views(probs_grouped[b], h, probs_words[b, h])
-            if h == 0:
+            if vector_regroups(b, h):
                 nc.vector.tensor_copy(out=to_sbuf, in_=from_psum)
             else:
                 nc.scalar.copy(out=to_sbuf, in_=from_psum)
@@ -155,36 +164,45 @@ def tile_quantumattentionblock_pb_t_kernel(tc, xwx, inp, V, x, out):
                 fold_second(s + 1)
             if live(s - 1):
                 regroup_probs(s - 1, 0)
+            if live(s - 1) and vector_regroups(s - 1, 1):
+                regroup_probs(s - 1, 1)
             if live(s + 1):
                 negated_row_max(s + 1)
             if live(s):
                 exponentials(s, 0)
                 exponentials(s, 1)
                 transpose_probs(s, 0)
-            if live(s - 1):
+            if live(s - 1) and not vector_regroups(s - 1, 1):
                 regroup_probs(s - 1, 1)
             if live(s):
                 exponentials(s, 2)
                 exponentials(s, 3)
                 transpose_probs(s, 1)
-                load_embeddings(s)
-                load_residual(s)
             if live(s) and live(s + SCORE_BUFFERS):
                 load_scores(s + SCORE_BUFFERS)
+            if live(s):
+                load_embeddings(s)
 
         def transpose_rows(rows):
             return [transpose_words(rows, h, words_psum, "words") for h in range(HALVES)]
 
-        def regroup_rows(banks):
+        def grouped_rows():
             grouped = ring2.tile([P, IMAGE_COLS], BF16, tag="rows_grouped", align_bytes=64)
-            for h in range(HALVES):
-                to_sbuf, from_psum = word_views(grouped, h, banks[h])
-                nc.vector.tensor_copy(out=to_sbuf, in_=from_psum)
             return grouped
 
-        def prepare_v():
-            grouped = regroup_rows(transpose_rows(v_rows))
-            nc.vector.quantize_mx(out=v_codes[:].bitcast(FP8X4), scales=v_scales[:], in_=grouped[:])
+        def regroup_rows(grouped, banks, h):
+            to_sbuf, from_psum = word_views(grouped, h, banks[h])
+            nc.vector.tensor_copy(out=to_sbuf, in_=from_psum)
+
+        def prepare_v(stage):
+            if stage == 0:
+                inp_words["V"] = transpose_rows(v_rows)
+            if stage == 1:
+                inp_grouped["V"] = grouped_rows()
+                for h in range(HALVES):
+                    regroup_rows(inp_grouped["V"], inp_words["V"], h)
+            if stage == 2:
+                nc.vector.quantize_mx(out=v_codes[:].bitcast(FP8X4), scales=v_scales[:], in_=inp_grouped["V"][:])
 
         def quantise_embeddings(b):
             codes = ring2.tile([P, SIDE], U32, tag="inp_codes", align_bytes=64)
@@ -245,7 +263,7 @@ def tile_quantumattentionblock_pb_t_kernel(tc, xwx, inp, V, x, out):
                     start=True,
                     stop=True,
                 )
-                result = ring4.tile([P, SIDE], F32, tag="result")
+                result = result_ring.tile([P, SIDE], F32, tag="result")
                 nc.vector.scalar_tensor_tensor(
                     out=result[:],
                     in0=bank[:],
@@ -264,13 +282,15 @@ def tile_quantumattentionblock_pb_t_kernel(tc, xwx, inp, V, x, out):
                 quantise_values(t - 1)
             if live(t + 1):
                 quantise_embeddings(t + 1)
+            if live(t + 2):
+                inp_grouped[t + 2] = grouped_rows()
             for h in range(HALVES):
+                if live(t + 2):
+                    regroup_rows(inp_grouped[t + 2], inp_words[t + 2], h)
                 if live(t - 1):
                     attend(t - 1, h)
                 if live(t + 1):
                     project(t + 1, h)
-            if live(t + 2):
-                inp_grouped[t + 2] = regroup_rows(inp_words[t + 2])
             if live(t + 3):
                 inp_words[t + 3] = transpose_rows(inp_rows[t + 3])
 
@@ -278,10 +298,11 @@ def tile_quantumattentionblock_pb_t_kernel(tc, xwx, inp, V, x, out):
             load_scores(b)
             if b == 1:
                 load_v()
-        for s in range(-1, 2 * IMAGES + 1):
+        for s in range(-1, VALUE_START + IMAGES + 1):
+            if live(s - RESIDUAL_STEP):
+                load_residual(s - RESIDUAL_STEP)
             softmax_step(s)
-            if s == 0:
-                prepare_v()
-            if s == IMAGES:
+            prepare_v(s + 1)
+            value_step(s - VALUE_START)
+            if s == IMAGES - 1:
                 nc.vector.reciprocal(out=inv_sum[:], in_=row_sum[:])
-            value_step(s - IMAGES)

@@ -30,6 +30,8 @@ RESULT_BUFFERS = 8
 FLOPS = IMAGES * 2 * (2 * SIDE * SIDE * SIDE)
 
 
+def DEFER(b):
+    return b == IMAGES - 2
 def tile_quantumattentionblock_pb_t_kernel(tc, xwx, inp, V, x, out):
     nc = tc.nc
     with ExitStack() as ctx:
@@ -49,6 +51,8 @@ def tile_quantumattentionblock_pb_t_kernel(tc, xwx, inp, V, x, out):
         make_identity(nc, ident_f32[:])
         eps = keep.tile([P, 1], F32)
         nc.vector.memset(eps[:], EPS)
+        warm = keep.tile([P, 1], F32)
+        nc.scalar.activation(out=warm[:], in_=eps[:], func=ACT.Exp)
 
         v_rows = keep.tile([P, IMAGE_COLS], BF16)
         v_codes = keep.tile([P, SIDE], U32, align_bytes=64)
@@ -68,7 +72,12 @@ def tile_quantumattentionblock_pb_t_kernel(tc, xwx, inp, V, x, out):
 
         def load_scores(b):
             rows = score_ring.tile([P, TILES, SIDE], BF16, tag="scores")
-            nc.sync.dma_start(out=rows[:], in_=xwx[b].rearrange("(p a) n -> p a n", a=TILES))
+            by_partition = xwx[b].rearrange("(p a) n -> p a n", a=TILES)
+            if b == 0:
+                for a in range(TILES):
+                    nc.sync.dma_start(out=rows[:, a, :], in_=by_partition[:, a, :])
+            else:
+                nc.sync.dma_start(out=rows[:], in_=by_partition)
             scores[b] = rows
 
         def load_residual(b):
@@ -103,24 +112,30 @@ def tile_quantumattentionblock_pb_t_kernel(tc, xwx, inp, V, x, out):
             as_words = grouped[:].bitcast(F32).rearrange("p (h i r u) -> p h i r u", h=HALVES, i=PER_HALF, u=2)
             return as_words[:, h], bank[:].rearrange("p i u r -> p i r u")
 
-        def fold_first(b):
-            half = ring2.tile([P, TILES, SIDE // 2], BF16, tag="fold_half")
+        def fold(b, width, rows=slice(0, TILES)):
+            wider = folded.get((b, 2 * width), scores[b])
+            if (b, width) not in folded:
+                narrower = ring2.tile([P, TILES, width], BF16, tag="fold_%d" % width)
+                folded[b, width] = narrower
             nc.vector.tensor_tensor(
-                out=half[:], in0=scores[b][:, :, : SIDE // 2], in1=scores[b][:, :, SIDE // 2 :], op=ALU.max
+                out=folded[b, width][:, rows, :], in0=wider[:, rows, :width], in1=wider[:, rows, width:], op=ALU.max
             )
-            folded[b] = half
 
-        def fold_second(b):
-            quarter = ring2.tile([P, TILES, SIDE // 4], BF16, tag="fold_quarter")
-            nc.vector.tensor_tensor(
-                out=quarter[:], in0=folded[b][:, :, : SIDE // 4], in1=folded[b][:, :, SIDE // 4 :], op=ALU.max
+        def negated_row_max(b, rows=slice(0, TILES)):
+            if b not in neg_max:
+                negated = ring3.tile([P, TILES], F32, tag="neg_max")
+                neg_max[b] = negated
+            nc.vector.tensor_reduce(
+                out=neg_max[b][:, rows], in_=folded[b, SIDE // 8][:, rows, :], axis=AXIS.X, op=ALU.max, negate=True
             )
-            folded[b] = quarter
 
-        def negated_row_max(b):
+        def first_row_max():
             negated = ring3.tile([P, TILES], F32, tag="neg_max")
-            nc.vector.tensor_reduce(out=negated[:], in_=folded[b][:], axis=AXIS.X, op=ALU.max, negate=True)
-            neg_max[b] = negated
+            for a in range(TILES):
+                nc.vector.tensor_reduce(
+                    out=negated[:, a : a + 1], in_=scores[0][:, a, :], axis=AXIS.X, op=ALU.max, negate=True
+                )
+            neg_max[0] = negated
 
         def exponentials(b, a):
             if a == 0:
@@ -138,7 +153,7 @@ def tile_quantumattentionblock_pb_t_kernel(tc, xwx, inp, V, x, out):
             probs_words[b, h] = transpose_words(probs[b], h, turn_psum, "turn")
 
         def vector_regroups(b, h):
-            return h == 0 or b % 3 == 2
+            return h == 0 or b > 8
 
         def regroup_probs(b, h):
             if h == 0:
@@ -156,17 +171,19 @@ def tile_quantumattentionblock_pb_t_kernel(tc, xwx, inp, V, x, out):
             )
 
         def softmax_step(s):
-            if live(s + 1):
-                fold_first(s + 1)
             if live(s - 2):
                 quantise_probs(s - 2)
-            if live(s + 1):
-                fold_second(s + 1)
+            if live(s + 1) and s > 0:
+                fold(s + 1, SIDE // 4)
             if live(s - 1):
                 regroup_probs(s - 1, 0)
+            if live(s + 1) and s > 0:
+                fold(s + 1, SIDE // 8)
             if live(s - 1) and vector_regroups(s - 1, 1):
                 regroup_probs(s - 1, 1)
-            if live(s + 1):
+            if live(s + 2):
+                fold(s + 2, SIDE // 2)
+            if live(s + 1) and s > 0:
                 negated_row_max(s + 1)
             if live(s):
                 exponentials(s, 0)
@@ -187,12 +204,15 @@ def tile_quantumattentionblock_pb_t_kernel(tc, xwx, inp, V, x, out):
             return [transpose_words(rows, h, words_psum, "words") for h in range(HALVES)]
 
         def grouped_rows():
-            grouped = ring2.tile([P, IMAGE_COLS], BF16, tag="rows_grouped", align_bytes=64)
+            grouped = ring3.tile([P, IMAGE_COLS], BF16, tag="rows_grouped", align_bytes=64)
             return grouped
 
-        def regroup_rows(grouped, banks, h):
+        def regroup_rows(grouped, banks, h, scalar_copies=False):
             to_sbuf, from_psum = word_views(grouped, h, banks[h])
-            nc.vector.tensor_copy(out=to_sbuf, in_=from_psum)
+            if scalar_copies:
+                nc.scalar.copy(out=to_sbuf, in_=from_psum)
+            else:
+                nc.vector.tensor_copy(out=to_sbuf, in_=from_psum)
 
         def prepare_v(stage):
             if stage == 0:
@@ -205,8 +225,8 @@ def tile_quantumattentionblock_pb_t_kernel(tc, xwx, inp, V, x, out):
                 nc.vector.quantize_mx(out=v_codes[:].bitcast(FP8X4), scales=v_scales[:], in_=inp_grouped["V"][:])
 
         def quantise_embeddings(b):
-            codes = ring2.tile([P, SIDE], U32, tag="inp_codes", align_bytes=64)
-            scales = ring2.tile([P, SIDE], U8, tag="inp_scales", align_bytes=64)
+            codes = ring3.tile([P, SIDE], U32, tag="inp_codes", align_bytes=64)
+            scales = ring3.tile([P, SIDE], U8, tag="inp_scales", align_bytes=64)
             nc.vector.quantize_mx(out=codes[:].bitcast(FP8X4), scales=scales[:], in_=inp_grouped[b][:])
             inp_mx[b] = (codes, scales)
 
@@ -226,20 +246,31 @@ def tile_quantumattentionblock_pb_t_kernel(tc, xwx, inp, V, x, out):
                     )
                 u_banks[b, c] = bank
 
-        def square(b):
-            squared = ring2.tile([P, TILES, P, PACK], F32, tag="squares")
-            for c in range(TILES):
-                nc.scalar.activation(
-                    out=squared[:, c], in_=u_banks[b, c][:].rearrange("p j d -> p d j"), func=ACT.Square
-                )
-            squares[b] = squared
+        def square(b, c):
+            if c == 0:
+                squared = ring2.tile([P, TILES, P, PACK], F32, tag="squares")
+                squares[b] = squared
+            nc.scalar.activation(
+                out=squares[b][:, c], in_=u_banks[b, c][:].rearrange("p j d -> p d j"), func=ACT.Square
+            )
 
-        def root(b):
-            grouped = ring2.tile([P, HALVES, IMAGE_COLS // HALVES], BF16, tag="vx_grouped", align_bytes=64)
+        def root(b, h):
+            if h == 0:
+                grouped = ring3.tile([P, HALVES, IMAGE_COLS // HALVES], BF16, tag="vx_grouped", align_bytes=64)
+                vx_grouped[b] = grouped
             flat = squares[b][:].rearrange("p (h c) d j -> p h (c d j)", h=HALVES)
-            for h in range(HALVES):
-                nc.scalar.activation(out=grouped[:, h, :], in_=flat[:, h, :], func=ACT.Sqrt, bias=eps[:, 0:1])
-            vx_grouped[b] = grouped
+            nc.scalar.activation(out=vx_grouped[b][:, h, :], in_=flat[:, h, :], func=ACT.Sqrt, bias=eps[:, 0:1])
+
+        def magnitudes(b):
+            for c in range(TILES - 1):
+                square(b, c)
+            if b == IMAGES - 1:
+                root(b, 0)
+                square(b, TILES - 1)
+            else:
+                square(b, TILES - 1)
+                root(b, 0)
+            root(b, 1)
 
         def quantise_values(b):
             codes = ring2.tile([P, SIDE], U32, tag="vx_codes", align_bytes=64)
@@ -249,11 +280,56 @@ def tile_quantumattentionblock_pb_t_kernel(tc, xwx, inp, V, x, out):
             )
             vx_mx[b] = (codes, scales)
 
+        def finish_quantise(h):
+            half = SIDE // HALVES
+            b = IMAGES - 1
+            codes = ring2.tile([P, half], U32, tag="vx_codes_half", align_bytes=64)
+            scales = ring2.tile([P, half], U8, tag="vx_scales_half", align_bytes=64)
+            nc.vector.quantize_mx(out=codes[:].bitcast(FP8X4), scales=scales[:], in_=vx_grouped[b][:, h, :])
+            vx_mx[b, h] = (codes, scales)
+
+        def finish_last(h, pair):
+            b = IMAGES - 1
+            half = SIDE // HALVES
+            codes, scales = vx_mx[b, h]
+            out_rows = out[b].rearrange("(p a) d -> p a d", a=TILES)
+            if True:
+                bank = u_psum.tile([P, PER_HALF, half], F32, tag="u")
+                result = result_ring.tile([P, PER_HALF, half], F32, tag="result")
+                for i in range(PER_HALF):
+                    a = pair * PER_HALF + i
+                    nc.tensor.matmul_mx(
+                        out=bank[:, i, :],
+                        lhsT=e_codes[:, b, a * P : (a + 1) * P].bitcast(FP8X4),
+                        lhsT_scale=e_scales[:, b, a * P : (a + 1) * P],
+                        rhs=codes[:].bitcast(FP8X4),
+                        rhs_scale=scales[:],
+                        start=True,
+                        stop=True,
+                    )
+                for i in range(PER_HALF):
+                    a = pair * PER_HALF + i
+                    nc.vector.scalar_tensor_tensor(
+                        out=result[:, i, :],
+                        in0=bank[:, i, :],
+                        scalar=inv_sum[:, TILES * b + a : TILES * b + a + 1],
+                        in1=x_rows[b][:, a, h * half : (h + 1) * half],
+                        op0=ALU.mult,
+                        op1=ALU.add,
+                    )
+                first = pair * PER_HALF
+                nc.sync.dma_start(
+                    out=out_rows[:, first : first + PER_HALF, h * half : (h + 1) * half], in_=result[:]
+                )
+
         def attend(b, h):
             codes, scales = vx_mx[b]
             out_rows = out[b].rearrange("(p a) d -> p a d", a=TILES)
             for a in range(h * PER_HALF, (h + 1) * PER_HALF):
-                bank = turn_psum.tile([P, SIDE], F32, tag="turn")
+                if h == 1 and DEFER(b):
+                    bank = words_psum.tile([P, SIDE], F32, tag="words")
+                else:
+                    bank = turn_psum.tile([P, SIDE], F32, tag="turn")
                 nc.tensor.matmul_mx(
                     out=bank[:],
                     lhsT=e_codes[:, b, a * P : (a + 1) * P].bitcast(FP8X4),
@@ -274,35 +350,58 @@ def tile_quantumattentionblock_pb_t_kernel(tc, xwx, inp, V, x, out):
                 )
                 nc.sync.dma_start(out=out_rows[:, a, :], in_=result[:])
 
+        def prepared(t):
+            return [t + 1] if t < 0 else [t + 1, t + 2] if t == 0 else [t + 2]
+
         def value_step(t):
             if live(t):
-                square(t)
-                root(t)
+                magnitudes(t)
+            if t == IMAGES:
+                finish_quantise(0)
+                if DEFER(t - 2):
+                    attend(t - 2, 1)
+                finish_last(0, 0)
+                finish_quantise(1)
+                finish_last(0, 1)
+                finish_last(1, 0)
+                finish_last(1, 1)
+                return
             if live(t - 1):
                 quantise_values(t - 1)
-            if live(t + 1):
-                quantise_embeddings(t + 1)
-            if live(t + 2):
-                inp_grouped[t + 2] = grouped_rows()
-            for h in range(HALVES):
-                if live(t + 2):
-                    regroup_rows(inp_grouped[t + 2], inp_words[t + 2], h)
-                if live(t - 1):
-                    attend(t - 1, h)
-                if live(t + 1):
-                    project(t + 1, h)
-            if live(t + 3):
-                inp_words[t + 3] = transpose_rows(inp_rows[t + 3])
+            if live(t - 2) and DEFER(t - 2):
+                attend(t - 2, 1)
+            for n, k in enumerate(prepared(t)):
+                if live(k):
+                    quantise_embeddings(k)
+                if live(k + 1):
+                    inp_grouped[k + 1] = grouped_rows()
+                for h in range(HALVES):
+                    if live(k + 1):
+                        regroup_rows(inp_grouped[k + 1], inp_words[k + 1], h, h == 1 and k + 1 == 5)
+                    if n == 0:
+                        if live(t - 1) and not (h == 1 and DEFER(t - 1)):
+                            attend(t - 1, h)
+                        if live(t + 1):
+                            project(t + 1, h)
+                if live(k + 2):
+                    inp_words[k + 2] = transpose_rows(inp_rows[k + 2])
 
         for b in range(SCORE_BUFFERS):
             load_scores(b)
             if b == 1:
                 load_v()
-        for s in range(-1, VALUE_START + IMAGES + 1):
+        first_row_max()
+        halves = [slice(0, 2), slice(2, 4)]
+        for w in (2, 4, 8):
+            for r in halves:
+                fold(1, SIDE // w, r)
+        for r in halves:
+            negated_row_max(1, r)
+        for s in range(VALUE_START + IMAGES + 1):
             if live(s - RESIDUAL_STEP):
                 load_residual(s - RESIDUAL_STEP)
             softmax_step(s)
-            prepare_v(s + 1)
+            prepare_v(s - 4)
             value_step(s - VALUE_START)
             if s == IMAGES - 1:
                 nc.vector.reciprocal(out=inv_sum[:], in_=row_sum[:])

@@ -153,7 +153,7 @@ def tile_quantumattentionblock_pb_t_kernel(tc, xwx, inp, V, x, out):
             probs_words[b, h] = transpose_words(probs[b], h, turn_psum, "turn")
 
         def vector_regroups(b, h):
-            return h == 0 or b > 8
+            return h == 0 or b > 8 or b == 2
 
         def regroup_probs(b, h):
             if h == 0:
@@ -179,12 +179,12 @@ def tile_quantumattentionblock_pb_t_kernel(tc, xwx, inp, V, x, out):
                 regroup_probs(s - 1, 0)
             if live(s + 1) and s > 0:
                 fold(s + 1, SIDE // 8)
-            if live(s - 1) and vector_regroups(s - 1, 1):
-                regroup_probs(s - 1, 1)
             if live(s + 2):
                 fold(s + 2, SIDE // 2)
             if live(s + 1) and s > 0:
                 negated_row_max(s + 1)
+            if live(s - 1) and vector_regroups(s - 1, 1):
+                regroup_probs(s - 1, 1)
             if live(s):
                 exponentials(s, 0)
                 exponentials(s, 1)
@@ -254,12 +254,17 @@ def tile_quantumattentionblock_pb_t_kernel(tc, xwx, inp, V, x, out):
                 out=squares[b][:, c], in_=u_banks[b, c][:].rearrange("p j d -> p d j"), func=ACT.Square
             )
 
-        def root(b, h):
+        def root(b, h, pieces=1):
             if h == 0:
                 grouped = ring3.tile([P, HALVES, IMAGE_COLS // HALVES], BF16, tag="vx_grouped", align_bytes=64)
                 vx_grouped[b] = grouped
             flat = squares[b][:].rearrange("p (h c) d j -> p h (c d j)", h=HALVES)
-            nc.scalar.activation(out=vx_grouped[b][:, h, :], in_=flat[:, h, :], func=ACT.Sqrt, bias=eps[:, 0:1])
+            width = IMAGE_COLS // HALVES // pieces
+            for i in range(pieces):
+                cols = slice(i * width, (i + 1) * width)
+                nc.scalar.activation(
+                    out=vx_grouped[b][:, h, cols], in_=flat[:, h, cols], func=ACT.Sqrt, bias=eps[:, 0:1]
+                )
 
         def magnitudes(b):
             for c in range(TILES - 1):
@@ -270,7 +275,7 @@ def tile_quantumattentionblock_pb_t_kernel(tc, xwx, inp, V, x, out):
             else:
                 square(b, TILES - 1)
                 root(b, 0)
-            root(b, 1)
+            root(b, 1, 2 if b == IMAGES - 1 else 1)
 
         def quantise_values(b):
             codes = ring2.tile([P, SIDE], U32, tag="vx_codes", align_bytes=64)
@@ -317,10 +322,7 @@ def tile_quantumattentionblock_pb_t_kernel(tc, xwx, inp, V, x, out):
                         op0=ALU.mult,
                         op1=ALU.add,
                     )
-                first = pair * PER_HALF
-                nc.sync.dma_start(
-                    out=out_rows[:, first : first + PER_HALF, h * half : (h + 1) * half], in_=result[:]
-                )
+                    nc.sync.dma_start(out=out_rows[:, a, h * half : (h + 1) * half], in_=result[:, i, :])
 
         def attend(b, h):
             codes, scales = vx_mx[b]
@@ -350,12 +352,41 @@ def tile_quantumattentionblock_pb_t_kernel(tc, xwx, inp, V, x, out):
                 )
                 nc.sync.dma_start(out=out_rows[:, a, :], in_=result[:])
 
-        def prepared(t):
-            return [t + 1] if t < 0 else [t + 1, t + 2] if t == 0 else [t + 2]
+        def begin_item(k):
+            if live(k):
+                quantise_embeddings(k)
+            if live(k + 1):
+                inp_grouped[k + 1] = grouped_rows()
+
+        def half_item(k, h):
+            if live(k + 1):
+                regroup_rows(inp_grouped[k + 1], inp_words[k + 1], h)
+
+        def end_item(k):
+            if live(k + 2):
+                inp_words[k + 2] = transpose_rows(inp_rows[k + 2])
 
         def value_step(t):
             if live(t):
                 magnitudes(t)
+            if t < 0:
+                begin_item(t + 1)
+                if live(t + 1):
+                    project(t + 1, 0)
+                    project(t + 1, 1)
+                half_item(t + 1, 0)
+                half_item(t + 1, 1)
+                end_item(t + 1)
+                return
+            if t == 0:
+                for k in range(1, 2 + 1):
+                    begin_item(k)
+                    half_item(k, 0)
+                    half_item(k, 1)
+                    end_item(k)
+                project(1, 0)
+                project(1, 1)
+                return
             if t == IMAGES:
                 finish_quantise(0)
                 if DEFER(t - 2):
@@ -366,29 +397,27 @@ def tile_quantumattentionblock_pb_t_kernel(tc, xwx, inp, V, x, out):
                 finish_last(1, 0)
                 finish_last(1, 1)
                 return
-            if live(t - 1):
-                quantise_values(t - 1)
-            if live(t - 2) and DEFER(t - 2):
+            quantise_values(t - 1)
+            if DEFER(t - 2):
                 attend(t - 2, 1)
-            for n, k in enumerate(prepared(t)):
-                if live(k):
-                    quantise_embeddings(k)
-                if live(k + 1):
-                    inp_grouped[k + 1] = grouped_rows()
-                for h in range(HALVES):
-                    if live(k + 1):
-                        regroup_rows(inp_grouped[k + 1], inp_words[k + 1], h, h == 1 and k + 1 == 5)
-                    if n == 0:
-                        if live(t - 1) and not (h == 1 and DEFER(t - 1)):
-                            attend(t - 1, h)
-                        if live(t + 1):
-                            project(t + 1, h)
-                if live(k + 2):
-                    inp_words[k + 2] = transpose_rows(inp_rows[k + 2])
+            k = t + 2
+            begin_item(k)
+            half_item(k, 0)
+            attend(t - 1, 0)
+            if live(t + 1):
+                project(t + 1, 0)
+            half_item(k, 1)
+            if t < 9 and live(t + 1):
+                project(t + 1, 1)
+            if not DEFER(t - 1):
+                attend(t - 1, 1)
+            if not t < 9 and live(t + 1):
+                project(t + 1, 1)
+            end_item(k)
 
         for b in range(SCORE_BUFFERS):
             load_scores(b)
-            if b == 1:
+            if b == 2:
                 load_v()
         first_row_max()
         halves = [slice(0, 2), slice(2, 4)]

@@ -153,7 +153,7 @@ def tile_quantumattentionblock_pb_t_kernel(tc, xwx, inp, V, x, out):
             probs_words[b, h] = transpose_words(probs[b], h, turn_psum, "turn")
 
         def vector_regroups(b, h):
-            return h == 0 or b > 8 or b == 2
+            return h == 0 or b > 9
 
         def regroup_probs(b, h):
             if h == 0:
@@ -360,7 +360,7 @@ def tile_quantumattentionblock_pb_t_kernel(tc, xwx, inp, V, x, out):
 
         def half_item(k, h):
             if live(k + 1):
-                regroup_rows(inp_grouped[k + 1], inp_words[k + 1], h)
+                regroup_rows(inp_grouped[k + 1], inp_words[k + 1], h, h == 1 and k + 1 in (5, 8))
 
         def end_item(k):
             if live(k + 2):

@@ -31,7 +31,7 @@ FLOPS = IMAGES * 2 * (2 * SIDE * SIDE * SIDE)
 
 
 def DEFER(b):
-    return b == IMAGES - 2
+    return b >= IMAGES - 3
 def tile_quantumattentionblock_pb_t_kernel(tc, xwx, inp, V, x, out):
     nc = tc.nc
     with ExitStack() as ctx:
@@ -43,9 +43,8 @@ def tile_quantumattentionblock_pb_t_kernel(tc, xwx, inp, V, x, out):
         result_ring = ctx.enter_context(tc.tile_pool(name="result_ring", bufs=RESULT_BUFFERS))
         ring3 = ctx.enter_context(tc.tile_pool(name="ring3", bufs=3))
         ring2 = ctx.enter_context(tc.tile_pool(name="ring2", bufs=2))
-        words_psum = ctx.enter_context(tc.psum_pool(name="words_psum", bufs=HALVES))
+        turn_psum = ctx.enter_context(tc.psum_pool(name="turn_psum", bufs=4))
         u_psum = ctx.enter_context(tc.psum_pool(name="u_psum", bufs=TILES))
-        turn_psum = ctx.enter_context(tc.psum_pool(name="turn_psum", bufs=2))
 
         ident_f32 = keep.tile([P, P], F32)
         make_identity(nc, ident_f32[:])
@@ -201,7 +200,7 @@ def tile_quantumattentionblock_pb_t_kernel(tc, xwx, inp, V, x, out):
                 load_embeddings(s)
 
         def transpose_rows(rows):
-            return [transpose_words(rows, h, words_psum, "words") for h in range(HALVES)]
+            return [transpose_words(rows, h, turn_psum, "turn") for h in range(HALVES)]
 
         def grouped_rows():
             grouped = ring3.tile([P, IMAGE_COLS], BF16, tag="rows_grouped", align_bytes=64)
@@ -328,10 +327,7 @@ def tile_quantumattentionblock_pb_t_kernel(tc, xwx, inp, V, x, out):
             codes, scales = vx_mx[b]
             out_rows = out[b].rearrange("(p a) d -> p a d", a=TILES)
             for a in range(h * PER_HALF, (h + 1) * PER_HALF):
-                if h == 1 and DEFER(b):
-                    bank = words_psum.tile([P, SIDE], F32, tag="words")
-                else:
-                    bank = turn_psum.tile([P, SIDE], F32, tag="turn")
+                bank = turn_psum.tile([P, SIDE], F32, tag="turn")
                 nc.tensor.matmul_mx(
                     out=bank[:],
                     lhsT=e_codes[:, b, a * P : (a + 1) * P].bitcast(FP8X4),
@@ -360,7 +356,7 @@ def tile_quantumattentionblock_pb_t_kernel(tc, xwx, inp, V, x, out):
 
         def half_item(k, h):
             if live(k + 1):
-                regroup_rows(inp_grouped[k + 1], inp_words[k + 1], h, h == 1 and k + 1 in (5, 8))
+                regroup_rows(inp_grouped[k + 1], inp_words[k + 1], h)
 
         def end_item(k):
             if live(k + 2):
@@ -403,15 +399,13 @@ def tile_quantumattentionblock_pb_t_kernel(tc, xwx, inp, V, x, out):
             k = t + 2
             begin_item(k)
             half_item(k, 0)
+            half_item(k, 1)
             attend(t - 1, 0)
             if live(t + 1):
                 project(t + 1, 0)
-            half_item(k, 1)
-            if t < 9 and live(t + 1):
-                project(t + 1, 1)
             if not DEFER(t - 1):
                 attend(t - 1, 1)
-            if not t < 9 and live(t + 1):
+            if live(t + 1):
                 project(t + 1, 1)
             end_item(k)
 

@@ -19,6 +19,7 @@ PACK = 4
 TILES = SIDE // P
 HALVES = 2
 PER_HALF = TILES // HALVES
+LATE = 1
 IMAGE_COLS = TILES * SIDE
 EPS = 1e-8
 SCORE_BUFFERS = 6
@@ -68,6 +69,12 @@ def tile_quantumattentionblock_pb_t_kernel(tc, xwx, inp, V, x, out):
 
         def live(b):
             return 0 <= b < IMAGES
+
+        def early(b):
+            return 0 <= b < IMAGES - LATE
+
+        def item(k):
+            return 0 <= k < IMAGES + LATE
 
         def load_scores(b):
             rows = score_ring.tile([P, TILES, SIDE], BF16, tag="scores")
@@ -152,7 +159,7 @@ def tile_quantumattentionblock_pb_t_kernel(tc, xwx, inp, V, x, out):
             probs_words[b, h] = transpose_words(probs[b], h, turn_psum, "turn")
 
         def vector_regroups(b, h):
-            return h == 0 or b > 9
+            return h == 0 or b > 8
 
         def regroup_probs(b, h):
             if h == 0:
@@ -170,11 +177,11 @@ def tile_quantumattentionblock_pb_t_kernel(tc, xwx, inp, V, x, out):
             )
 
         def softmax_step(s):
-            if live(s - 2):
+            if early(s - 2):
                 quantise_probs(s - 2)
             if live(s + 1) and s > 0:
                 fold(s + 1, SIDE // 4)
-            if live(s - 1):
+            if early(s - 1):
                 regroup_probs(s - 1, 0)
             if live(s + 1) and s > 0:
                 fold(s + 1, SIDE // 8)
@@ -182,18 +189,20 @@ def tile_quantumattentionblock_pb_t_kernel(tc, xwx, inp, V, x, out):
                 fold(s + 2, SIDE // 2)
             if live(s + 1) and s > 0:
                 negated_row_max(s + 1)
-            if live(s - 1) and vector_regroups(s - 1, 1):
+            if early(s - 1) and vector_regroups(s - 1, 1):
                 regroup_probs(s - 1, 1)
             if live(s):
                 exponentials(s, 0)
                 exponentials(s, 1)
-                transpose_probs(s, 0)
-            if live(s - 1) and not vector_regroups(s - 1, 1):
+                if early(s):
+                    transpose_probs(s, 0)
+            if early(s - 1) and not vector_regroups(s - 1, 1):
                 regroup_probs(s - 1, 1)
             if live(s):
                 exponentials(s, 2)
                 exponentials(s, 3)
-                transpose_probs(s, 1)
+                if early(s):
+                    transpose_probs(s, 1)
             if live(s) and live(s + SCORE_BUFFERS):
                 load_scores(s + SCORE_BUFFERS)
             if live(s):
@@ -224,6 +233,10 @@ def tile_quantumattentionblock_pb_t_kernel(tc, xwx, inp, V, x, out):
                 nc.vector.quantize_mx(out=v_codes[:].bitcast(FP8X4), scales=v_scales[:], in_=inp_grouped["V"][:])
 
         def quantise_embeddings(b):
+            if b >= IMAGES:
+                e = b - LATE
+                nc.vector.quantize_mx(out=e_codes[:, e, :].bitcast(FP8X4), scales=e_scales[:, e, :], in_=inp_grouped[b][:])
+                return
             codes = ring3.tile([P, SIDE], U32, tag="inp_codes", align_bytes=64)
             scales = ring3.tile([P, SIDE], U8, tag="inp_scales", align_bytes=64)
             nc.vector.quantize_mx(out=codes[:].bitcast(FP8X4), scales=scales[:], in_=inp_grouped[b][:])
@@ -349,18 +362,18 @@ def tile_quantumattentionblock_pb_t_kernel(tc, xwx, inp, V, x, out):
                 nc.sync.dma_start(out=out_rows[:, a, :], in_=result[:])
 
         def begin_item(k):
-            if live(k):
+            if item(k):
                 quantise_embeddings(k)
-            if live(k + 1):
+            if item(k + 1):
                 inp_grouped[k + 1] = grouped_rows()
 
         def half_item(k, h):
-            if live(k + 1):
+            if item(k + 1):
                 regroup_rows(inp_grouped[k + 1], inp_words[k + 1], h)
 
         def end_item(k):
-            if live(k + 2):
-                inp_words[k + 2] = transpose_rows(inp_rows[k + 2])
+            if item(k + 2):
+                inp_words[k + 2] = transpose_rows(inp_rows[k + 2] if k + 2 < IMAGES else probs[k + 2 - LATE])
 
         def value_step(t):
             if live(t):
@@ -384,6 +397,7 @@ def tile_quantumattentionblock_pb_t_kernel(tc, xwx, inp, V, x, out):
                 project(1, 1)
                 return
             if t == IMAGES:
+                begin_item(t + 2)
                 finish_quantise(0)
                 if DEFER(t - 2):
                     attend(t - 2, 1)

@@ -135,13 +135,20 @@ def tile_quantumattentionblock_pb_t_kernel(tc, xwx, inp, V, x, out):
                 out=neg_max[b][:, rows], in_=folded[b, SIDE // 8][:, rows, :], axis=AXIS.X, op=ALU.max, negate=True
             )
 
-        def first_row_max():
+        def row_max_by_tiles(b):
             negated = ring3.tile([P, TILES], F32, tag="neg_max")
             for a in range(TILES):
-                nc.vector.tensor_reduce(
-                    out=negated[:, a : a + 1], in_=scores[0][:, a, :], axis=AXIS.X, op=ALU.max, negate=True
+                flipped = ring2.tile([P, SIDE], BF16, tag="flipped")
+                nc.vector.tensor_scalar(
+                    out=flipped[:],
+                    in0=scores[b][:, a, :],
+                    scalar1=-1.0,
+                    scalar2=None,
+                    op0=ALU.mult,
+                    op1=ALU.min,
+                    accum_out=negated[:, a : a + 1],
                 )
-            neg_max[0] = negated
+            neg_max[b] = negated
 
         def exponentials(b, a):
             if a == 0:
@@ -179,15 +186,15 @@ def tile_quantumattentionblock_pb_t_kernel(tc, xwx, inp, V, x, out):
         def softmax_step(s):
             if early(s - 2):
                 quantise_probs(s - 2)
-            if live(s + 1) and s > 0:
+            if live(s + 1) and s + 1 >= 3:
                 fold(s + 1, SIDE // 4)
             if early(s - 1):
                 regroup_probs(s - 1, 0)
-            if live(s + 1) and s > 0:
+            if live(s + 1) and s + 1 >= 3:
                 fold(s + 1, SIDE // 8)
-            if live(s + 2):
+            if live(s + 2) and s + 2 >= 3:
                 fold(s + 2, SIDE // 2)
-            if live(s + 1) and s > 0:
+            if live(s + 1) and s + 1 >= 3:
                 negated_row_max(s + 1)
             if early(s - 1) and vector_regroups(s - 1, 1):
                 regroup_probs(s - 1, 1)
@@ -425,15 +432,11 @@ def tile_quantumattentionblock_pb_t_kernel(tc, xwx, inp, V, x, out):
 
         for b in range(SCORE_BUFFERS):
             load_scores(b)
-            if b == 2:
+            if b == 3:
                 load_v()
-        first_row_max()
-        halves = [slice(0, 2), slice(2, 4)]
-        for w in (2, 4, 8):
-            for r in halves:
-                fold(1, SIDE // w, r)
-        for r in halves:
-            negated_row_max(1, r)
+        row_max_by_tiles(0)
+        row_max_by_tiles(1)
+        row_max_by_tiles(2)
         for s in range(VALUE_START + IMAGES + 1):
             if live(s - RESIDUAL_STEP):
                 load_residual(s - RESIDUAL_STEP)

from contextlib import ExitStack

import concourse.mybir as mybir
from concourse.masks import make_identity

BF16 = mybir.dt.bfloat16
F32 = mybir.dt.float32
U32 = mybir.dt.uint32
U8 = mybir.dt.uint8
FP8X4 = mybir.dt.float8_e4m3fn_x4
ACT = mybir.ActivationFunctionType
ALU = mybir.AluOpType
AXIS = mybir.AxisListType

IMAGES = 12
SIDE = 512
P = 128
PACK = 4
TILES = SIDE // P
HALVES = 2
PER_HALF = TILES // HALVES
LATE = 1
IMAGE_COLS = TILES * SIDE
EPS = 1e-8
SCORE_BUFFERS = 6
RESIDUAL_BUFFERS = 6
RESIDUAL_STEP = 8
VALUE_START = IMAGES - 1
RESULT_BUFFERS = 8

FLOPS = IMAGES * 2 * (2 * SIDE * SIDE * SIDE)


def DEFER(b):
    return b >= IMAGES - 3
def tile_quantumattentionblock_pb_t_kernel(tc, xwx, inp, V, x, out):
    nc = tc.nc
    with ExitStack() as ctx:
        ctx.enter_context(tc.manual_schedule())
        keep = ctx.enter_context(tc.tile_pool(name="keep", bufs=1))
        resident = ctx.enter_context(tc.tile_pool(name="resident", bufs=IMAGES))
        score_ring = ctx.enter_context(tc.tile_pool(name="score_ring", bufs=SCORE_BUFFERS))
        residual_ring = ctx.enter_context(tc.tile_pool(name="residual_ring", bufs=RESIDUAL_BUFFERS))
        result_ring = ctx.enter_context(tc.tile_pool(name="result_ring", bufs=RESULT_BUFFERS))
        ring3 = ctx.enter_context(tc.tile_pool(name="ring3", bufs=3))
        ring2 = ctx.enter_context(tc.tile_pool(name="ring2", bufs=2))
        turn_psum = ctx.enter_context(tc.psum_pool(name="turn_psum", bufs=4))
        u_psum = ctx.enter_context(tc.psum_pool(name="u_psum", bufs=TILES))

        ident_f32 = keep.tile([P, P], F32)
        make_identity(nc, ident_f32[:])
        eps = keep.tile([P, 1], F32)
        nc.vector.memset(eps[:], EPS)
        warm = keep.tile([P, 1], F32)
        nc.scalar.activation(out=warm[:], in_=eps[:], func=ACT.Exp)

        v_rows = keep.tile([P, IMAGE_COLS], BF16)
        v_codes = keep.tile([P, SIDE], U32, align_bytes=64)
        v_scales = keep.tile([P, SIDE], U8, align_bytes=64)
        e_codes = keep.tile([P, IMAGES, SIDE], U32, align_bytes=64)
        e_scales = keep.tile([P, IMAGES, SIDE], U8, align_bytes=64)
        row_sum = keep.tile([P, IMAGES * TILES], F32)
        inv_sum = keep.tile([P, IMAGES * TILES], F32)

        scores, folded, neg_max, probs = {}, {}, {}, {}
        probs_words, probs_grouped = {}, {}
        inp_rows, x_rows, inp_words, inp_grouped, inp_mx = {}, {}, {}, {}, {}
        u_banks, squares, vx_grouped, vx_mx = {}, {}, {}, {}

        def live(b):
            return 0 <= b < IMAGES

        def early(b):
            return 0 <= b < IMAGES - LATE

        def item(k):
            return 0 <= k < IMAGES + LATE

        def load_scores(b):
            rows = score_ring.tile([P, TILES, SIDE], BF16, tag="scores")
            by_partition = xwx[b].rearrange("(p a) n -> p a n", a=TILES)
            if b == 0:
                for a in range(TILES):
                    nc.sync.dma_start(out=rows[:, a, :], in_=by_partition[:, a, :])
            else:
                nc.sync.dma_start(out=rows[:], in_=by_partition)
            scores[b] = rows

        def load_residual(b):
            rows = residual_ring.tile([P, TILES, SIDE], BF16, tag="x_rows")
            nc.sync.dma_start(out=rows[:], in_=x[b].rearrange("(p a) d -> p a d", a=TILES))
            x_rows[b] = rows

        def load_embeddings(b):
            rows = resident.tile([P, IMAGE_COLS], BF16, tag="inp_rows")
            nc.sync.dma_start(
                out=rows[:].rearrange("p (u c) -> p u c", u=2),
                in_=inp[b].rearrange("(u p e) f -> p u (e f)", u=2, e=2),
            )
            inp_rows[b] = rows

        def load_v():
            nc.sync.dma_start(
                out=v_rows[:].rearrange("p (c f) -> p c f", c=TILES),
                in_=V.rearrange("(c p) f -> p c f", p=P),
            )

        def transpose_words(rows, h, pool, tag):
            words = rows[:].bitcast(F32)
            bank = pool.tile([P, PER_HALF, 2, P], F32, tag=tag)
            for i in range(PER_HALF):
                for u in range(2):
                    first = ((h * PER_HALF + i) * 2 + u) * P
                    nc.tensor.transpose(bank[:, i, u, :], words[:, first : first + P], ident_f32[:])
            return bank

        def word_views(grouped, h, bank):
            as_words = grouped[:].bitcast(F32).rearrange("p (h i r u) -> p h i r u", h=HALVES, i=PER_HALF, u=2)
            return as_words[:, h], bank[:].rearrange("p i u r -> p i r u")

        def fold(b, width, rows=slice(0, TILES)):
            wider = folded.get((b, 2 * width), scores[b])
            if (b, width) not in folded:
                narrower = ring2.tile([P, TILES, width], BF16, tag="fold_%d" % width)
                folded[b, width] = narrower
            nc.vector.tensor_tensor(
                out=folded[b, width][:, rows, :], in0=wider[:, rows, :width], in1=wider[:, rows, width:], op=ALU.max
            )

        def negated_row_max(b, rows=slice(0, TILES)):
            if b not in neg_max:
                negated = ring3.tile([P, TILES], F32, tag="neg_max")
                neg_max[b] = negated
            nc.vector.tensor_reduce(
                out=neg_max[b][:, rows], in_=folded[b, SIDE // 8][:, rows, :], axis=AXIS.X, op=ALU.max, negate=True
            )

        def row_max_by_tiles(b):
            negated = ring3.tile([P, TILES], F32, tag="neg_max")
            for a in range(TILES):
                flipped = ring2.tile([P, SIDE], BF16, tag="flipped")
                nc.vector.tensor_scalar(
                    out=flipped[:],
                    in0=scores[b][:, a, :],
                    scalar1=-1.0,
                    scalar2=None,
                    op0=ALU.mult,
                    op1=ALU.min,
                    accum_out=negated[:, a : a + 1],
                )
            neg_max[b] = negated

        def exponentials(b, a):
            if a == 0:
                e_rows = ring2.tile([P, IMAGE_COLS], BF16, tag="probs")
                probs[b] = e_rows
            nc.scalar.activation(
                out=probs[b][:, a * SIDE : (a + 1) * SIDE],
                in_=scores[b][:, a, :],
                func=ACT.Exp,
                bias=neg_max[b][:, a : a + 1],
                accum_out=row_sum[:, TILES * b + a : TILES * b + a + 1],
            )

        def transpose_probs(b, h):
            probs_words[b, h] = transpose_words(probs[b], h, turn_psum, "turn")

        def vector_regroups(b, h):
            return h == 0 or b > 8

        def regroup_probs(b, h):
            if h == 0:
                grouped = ring2.tile([P, IMAGE_COLS], BF16, tag="probs_grouped", align_bytes=64)
                probs_grouped[b] = grouped
            to_sbuf, from_psum = word_views(probs_grouped[b], h, probs_words[b, h])
            if vector_regroups(b, h):
                nc.vector.tensor_copy(out=to_sbuf, in_=from_psum)
            else:
                nc.scalar.copy(out=to_sbuf, in_=from_psum)

        def quantise_probs(b):
            nc.vector.quantize_mx(
                out=e_codes[:, b, :].bitcast(FP8X4), scales=e_scales[:, b, :], in_=probs_grouped[b][:]
            )

        def softmax_step(s):
            if early(s - 2):
                quantise_probs(s - 2)
            if live(s + 1) and s + 1 >= 3:
                fold(s + 1, SIDE // 4)
            if early(s - 1):
                regroup_probs(s - 1, 0)
            if live(s + 1) and s + 1 >= 3:
                fold(s + 1, SIDE // 8)
            if live(s + 2) and s + 2 >= 3:
                fold(s + 2, SIDE // 2)
            if live(s + 1) and s + 1 >= 3:
                negated_row_max(s + 1)
            if early(s - 1) and vector_regroups(s - 1, 1):
                regroup_probs(s - 1, 1)
            if live(s):
                exponentials(s, 0)
                exponentials(s, 1)
                if early(s):
                    transpose_probs(s, 0)
            if early(s - 1) and not vector_regroups(s - 1, 1):
                regroup_probs(s - 1, 1)
            if live(s):
                exponentials(s, 2)
                exponentials(s, 3)
                if early(s):
                    transpose_probs(s, 1)
            if live(s) and live(s + SCORE_BUFFERS):
                load_scores(s + SCORE_BUFFERS)
            if live(s):
                load_embeddings(s)

        def transpose_rows(rows):
            return [transpose_words(rows, h, turn_psum, "turn") for h in range(HALVES)]

        def grouped_rows():
            grouped = ring3.tile([P, IMAGE_COLS], BF16, tag="rows_grouped", align_bytes=64)
            return grouped

        def regroup_rows(grouped, banks, h, scalar_copies=False):
            to_sbuf, from_psum = word_views(grouped, h, banks[h])
            if scalar_copies:
                nc.scalar.copy(out=to_sbuf, in_=from_psum)
            else:
                nc.vector.tensor_copy(out=to_sbuf, in_=from_psum)

        def prepare_v(stage):
            if stage == 0:
                inp_words["V"] = transpose_rows(v_rows)
            if stage == 1:
                inp_grouped["V"] = grouped_rows()
                for h in range(HALVES):
                    regroup_rows(inp_grouped["V"], inp_words["V"], h)
            if stage == 2:
                nc.vector.quantize_mx(out=v_codes[:].bitcast(FP8X4), scales=v_scales[:], in_=inp_grouped["V"][:])

        def quantise_embeddings(b):
            if b >= IMAGES:
                e = b - LATE
                nc.vector.quantize_mx(out=e_codes[:, e, :].bitcast(FP8X4), scales=e_scales[:, e, :], in_=inp_grouped[b][:])
                return
            codes = ring3.tile([P, SIDE], U32, tag="inp_codes", align_bytes=64)
            scales = ring3.tile([P, SIDE], U8, tag="inp_scales", align_bytes=64)
            nc.vector.quantize_mx(out=codes[:].bitcast(FP8X4), scales=scales[:], in_=inp_grouped[b][:])
            inp_mx[b] = (codes, scales)

        def project(b, h):
            codes, scales = inp_mx[b]
            for c in range(h * PER_HALF, (h + 1) * PER_HALF):
                bank = u_psum.tile([P, PACK, P], F32, tag="u")
                for j in range(PACK):
                    nc.tensor.matmul_mx(
                        out=bank[:, j, :],
                        lhsT=codes[:, j * P : (j + 1) * P].bitcast(FP8X4),
                        lhsT_scale=scales[:, j * P : (j + 1) * P],
                        rhs=v_codes[:, c * P : (c + 1) * P].bitcast(FP8X4),
                        rhs_scale=v_scales[:, c * P : (c + 1) * P],
                        start=True,
                        stop=True,
                    )
                u_banks[b, c] = bank

        def square(b, c):
            if c == 0:
                squared = ring2.tile([P, TILES, P, PACK], F32, tag="squares")
                squares[b] = squared
            nc.scalar.activation(
                out=squares[b][:, c], in_=u_banks[b, c][:].rearrange("p j d -> p d j"), func=ACT.Square
            )

        def root(b, h, pieces=1):
            if h == 0:
                grouped = ring3.tile([P, HALVES, IMAGE_COLS // HALVES], BF16, tag="vx_grouped", align_bytes=64)
                vx_grouped[b] = grouped
            flat = squares[b][:].rearrange("p (h c) d j -> p h (c d j)", h=HALVES)
            width = IMAGE_COLS // HALVES // pieces
            for i in range(pieces):
                cols = slice(i * width, (i + 1) * width)
                nc.scalar.activation(
                    out=vx_grouped[b][:, h, cols], in_=flat[:, h, cols], func=ACT.Sqrt, bias=eps[:, 0:1]
                )

        def magnitudes(b):
            for c in range(TILES - 1):
                square(b, c)
            if b == IMAGES - 1:
                root(b, 0)
                square(b, TILES - 1)
            else:
                square(b, TILES - 1)
                root(b, 0)
            root(b, 1, 2 if b == IMAGES - 1 else 1)

        def quantise_values(b):
            codes = ring2.tile([P, SIDE], U32, tag="vx_codes", align_bytes=64)
            scales = ring2.tile([P, SIDE], U8, tag="vx_scales", align_bytes=64)
            nc.vector.quantize_mx(
                out=codes[:].bitcast(FP8X4), scales=scales[:], in_=vx_grouped[b][:].rearrange("p h c -> p (h c)")
            )
            vx_mx[b] = (codes, scales)

        def finish_quantise(h):
            half = SIDE // HALVES
            b = IMAGES - 1
            codes = ring2.tile([P, half], U32, tag="vx_codes_half", align_bytes=64)
            scales = ring2.tile([P, half], U8, tag="vx_scales_half", align_bytes=64)
            nc.vector.quantize_mx(out=codes[:].bitcast(FP8X4), scales=scales[:], in_=vx_grouped[b][:, h, :])
            vx_mx[b, h] = (codes, scales)

        def finish_last(h, pair):
            b = IMAGES - 1
            half = SIDE // HALVES
            codes, scales = vx_mx[b, h]
            out_rows = out[b].rearrange("(p a) d -> p a d", a=TILES)
            if True:
                bank = u_psum.tile([P, PER_HALF, half], F32, tag="u")
                result = result_ring.tile([P, PER_HALF, half], F32, tag="result")
                for i in range(PER_HALF):
                    a = pair * PER_HALF + i
                    nc.tensor.matmul_mx(
                        out=bank[:, i, :],
                        lhsT=e_codes[:, b, a * P : (a + 1) * P].bitcast(FP8X4),
                        lhsT_scale=e_scales[:, b, a * P : (a + 1) * P],
                        rhs=codes[:].bitcast(FP8X4),
                        rhs_scale=scales[:],
                        start=True,
                        stop=True,
                    )
                for i in range(PER_HALF):
                    a = pair * PER_HALF + i
                    nc.vector.scalar_tensor_tensor(
                        out=result[:, i, :],
                        in0=bank[:, i, :],
                        scalar=inv_sum[:, TILES * b + a : TILES * b + a + 1],
                        in1=x_rows[b][:, a, h * half : (h + 1) * half],
                        op0=ALU.mult,
                        op1=ALU.add,
                    )
                    nc.sync.dma_start(out=out_rows[:, a, h * half : (h + 1) * half], in_=result[:, i, :])

        def attend(b, h):
            codes, scales = vx_mx[b]
            out_rows = out[b].rearrange("(p a) d -> p a d", a=TILES)
            for a in range(h * PER_HALF, (h + 1) * PER_HALF):
                bank = turn_psum.tile([P, SIDE], F32, tag="turn")
                nc.tensor.matmul_mx(
                    out=bank[:],
                    lhsT=e_codes[:, b, a * P : (a + 1) * P].bitcast(FP8X4),
                    lhsT_scale=e_scales[:, b, a * P : (a + 1) * P],
                    rhs=codes[:].bitcast(FP8X4),
                    rhs_scale=scales[:],
                    start=True,
                    stop=True,
                )
                result = result_ring.tile([P, SIDE], F32, tag="result")
                nc.vector.scalar_tensor_tensor(
                    out=result[:],
                    in0=bank[:],
                    scalar=inv_sum[:, TILES * b + a : TILES * b + a + 1],
                    in1=x_rows[b][:, a, :],
                    op0=ALU.mult,
                    op1=ALU.add,
                )
                nc.sync.dma_start(out=out_rows[:, a, :], in_=result[:])

        def begin_item(k):
            if item(k):
                quantise_embeddings(k)
            if item(k + 1):
                inp_grouped[k + 1] = grouped_rows()

        def half_item(k, h):
            if item(k + 1):
                regroup_rows(inp_grouped[k + 1], inp_words[k + 1], h)

        def end_item(k):
            if item(k + 2):
                inp_words[k + 2] = transpose_rows(inp_rows[k + 2] if k + 2 < IMAGES else probs[k + 2 - LATE])

        def value_step(t):
            if live(t):
                magnitudes(t)
            if t < 0:
                begin_item(t + 1)
                if live(t + 1):
                    project(t + 1, 0)
                    project(t + 1, 1)
                half_item(t + 1, 0)
                half_item(t + 1, 1)
                end_item(t + 1)
                return
            if t == 0:
                for k in range(1, 2 + 1):
                    begin_item(k)
                    half_item(k, 0)
                    half_item(k, 1)
                    end_item(k)
                project(1, 0)
                project(1, 1)
                return
            if t == IMAGES:
                begin_item(t + 2)
                finish_quantise(0)
                if DEFER(t - 2):
                    attend(t - 2, 1)
                finish_last(0, 0)
                finish_quantise(1)
                finish_last(0, 1)
                finish_last(1, 0)
                finish_last(1, 1)
                return
            quantise_values(t - 1)
            if DEFER(t - 2):
                attend(t - 2, 1)
            k = t + 2
            begin_item(k)
            half_item(k, 0)
            half_item(k, 1)
            attend(t - 1, 0)
            if live(t + 1):
                project(t + 1, 0)
            if not DEFER(t - 1):
                attend(t - 1, 1)
            if live(t + 1):
                project(t + 1, 1)
            end_item(k)

        for b in range(SCORE_BUFFERS):
            load_scores(b)
            if b == 3:
                load_v()
        row_max_by_tiles(0)
        row_max_by_tiles(1)
        row_max_by_tiles(2)
        for s in range(VALUE_START + IMAGES + 1):
            if live(s - RESIDUAL_STEP):
                load_residual(s - RESIDUAL_STEP)
            softmax_step(s)
            prepare_v(s - 4)
            value_step(s - VALUE_START)
            if s == IMAGES - 1:
                nc.vector.reciprocal(out=inv_sum[:], in_=row_sum[:])
